import numpy as np
import ml_dtypes


def mxq(x, axis, fmt="e4m3"):
    dtype, down = {"e4m3": (ml_dtypes.float8_e4m3fn, 7), "e5m2": (ml_dtypes.float8_e5m2, 14)}[fmt]
    v = np.moveaxis(np.asarray(x, np.float32).astype(ml_dtypes.bfloat16).astype(np.float64), axis, -1)
    blocks = v.reshape(v.shape[:-1] + (-1, 32))
    amax = np.abs(blocks).max(-1, keepdims=True)
    byte = np.maximum(np.where(amax > 0, np.frexp(amax)[1] - 1 + 127, 0) - down, 1)
    scale = np.exp2(byte - 127.0)
    codes = (blocks / scale).astype(np.float32).astype(dtype).astype(np.float64)
    return np.moveaxis((codes * scale).reshape(v.shape), -1, axis)


WIDE = False


def mx_kscale(k):
    if not WIDE:
        return np.ones(k)
    levels = np.array([10, -10, 5, -5, 0])
    a = np.random.permutation(np.resize(levels, k // 512 * 4)).reshape(k // 512, 4)
    idx = np.arange(k)
    return np.exp2(a[idx // 512, idx % 128 // 32])


BF16 = ml_dtypes.bfloat16


def bf(x):
    return np.asarray(x, np.float32).astype(BF16)


def f64(x):
    return np.asarray(x).astype(np.float64)


E2M1 = np.array([0.0, 0.5, 1.0, 1.5, 2.0, 3.0, 4.0, 6.0, -0.0, -0.5, -1.0, -1.5, -2.0, -3.0, -4.0, -6.0])


def pack_weight(w, fmt):
    k, n = w.shape
    w = f64(bf(w)).reshape(k // 32, 32, n)
    amax = np.abs(w).max(1)
    if fmt == "e4m3":
        byte = np.frexp(amax)[1] - 1 + 127 - 7
    else:
        mant, ex = np.frexp(amax / 6.0)
        byte = np.where(mant > 0.5, ex, ex - 1) + 127
    byte = np.clip(np.where(amax > 0, byte, 1), 1, 254)
    scaled = (w * np.exp2(127.0 - byte)[:, None, :]).reshape(k, n).astype(np.float32)
    by_word = np.ascontiguousarray(scaled.reshape(k // 512, 128, 4, n).transpose(0, 1, 3, 2))
    if fmt == "e4m3":
        words = by_word.astype(ml_dtypes.float8_e4m3fn).view(np.uint8)
    else:
        c = by_word.astype(ml_dtypes.float4_e2m1fn).view(np.uint8) & 0xF
        words = c[..., 0::2] | (c[..., 1::2] << 4)
    return np.ascontiguousarray(words), np.ascontiguousarray(byte.astype(np.uint8).reshape(k // 512, 16, n))


def unpack_weight(words, scales, fmt):
    g, p, n, _ = words.shape
    if fmt == "e4m3":
        vals = np.ascontiguousarray(words).view(ml_dtypes.float8_e4m3fn).astype(np.float64)
    else:
        nib = np.empty((g, p, n, 4), np.uint8)
        nib[..., 0::2] = words & 0xF
        nib[..., 1::2] = words >> 4
        vals = E2M1[nib]
    vals = vals * np.repeat(np.exp2(scales.astype(np.float64) - 127.0), 8, axis=1)[..., None]
    return vals.transpose(0, 1, 3, 2).reshape(g * 512, n)

def pack4(w):
    words, scales = pack_weight(w, "e2m1")
    return words.reshape(words.shape[0], 128, -1), scales


def unpack4(words, scales):
    return unpack_weight(words.reshape(words.shape[0], 128, -1, 2), scales, "e2m1")


B, CIN, CMID, C4, C8, COUT, T, H, W = 2, 256, 8192, 256, 128, 128, 4, 16, 16
S = T * H * W


def setup_inputs():
    s = mx_kscale(CMID)
    h_add = np.maximum(np.random.standard_normal((B, CMID, S)) * np.sqrt(2.0), 0.0)
    h_occ = np.maximum(np.random.standard_normal((B, C8, S)) * np.sqrt(2.0), 0.0)
    w_add2 = np.random.standard_normal((CIN, CMID)) * np.sqrt(2.0 / CMID) / s[None, :]
    words, scales = pack4(np.ascontiguousarray(w_add2.T))
    return {"h_add": bf(h_add * s[None, :, None]),
            "w_add2_words": words,
            "w_add2_scales": scales,
            "b_add2": bf(np.random.standard_normal(CIN) * 0.3),
            "h_occ": bf(h_occ),
            "w_occ3": bf(np.random.standard_normal((COUT, C8)) / np.sqrt(C8))}


def reference(h_add, w_add2_words, w_add2_scales, b_add2, h_occ, w_occ3):
    feat = (unpack4(w_add2_words, w_add2_scales).T @ mxq(f64(h_add), 1, "e4m3")) + f64(b_add2)[None, :, None]
    occ = np.abs(f64(w_occ3) @ f64(h_occ))
    return (mxq(occ, 2, "e4m3") @ mxq(feat, 2, "e4m3").transpose(0, 2, 1)) / S

@@ -1,0 +1,246 @@
+from contextlib import ExitStack
+
+import concourse.mybir as mybir
+from concourse.masks import make_identity
+
+BF16 = mybir.dt.bfloat16
+F32 = mybir.dt.float32
+I32 = mybir.dt.int32
+U32 = mybir.dt.uint32
+U8 = mybir.dt.uint8
+FP8X4 = mybir.dt.float8_e4m3fn_x4
+FP4X4 = mybir.dt.float4_e2m1fn_x4
+ACT = mybir.ActivationFunctionType
+
+P = 128
+PACK = 4
+K_PASS = P * PACK
+BANK = 512
+
+SAMPLES = 2
+CHANNELS = 8192
+VOXELS = 1024
+FEATS = 256
+MAPS = 128
+GROUPS = CHANNELS // K_PASS
+HALVES = VOXELS // BANK
+FEAT_TILES = FEATS // P
+RUN = 4
+WEIGHT_LOADS = 4
+RAW_BUFS = 8
+
+FLOPS = 2 * SAMPLES * VOXELS * (FEATS * CHANNELS + MAPS * P + MAPS * FEATS)
+
+
+def tile_occurrencepool_pa_k_kernel(
+    tc, h_add, w_add2_words, w_add2_scales, b_add2, h_occ, w_occ3, out
+):
+    nc = tc.nc
+    with ExitStack() as stack:
+        stack.enter_context(tc.manual_schedule())
+        keep = stack.enter_context(tc.tile_pool(name="keep", bufs=1))
+        raw_pool = stack.enter_context(tc.tile_pool(name="raw", bufs=RAW_BUFS))
+        chunk_pool = stack.enter_context(tc.tile_pool(name="chunk", bufs=3))
+        sample_pool = stack.enter_context(tc.tile_pool(name="sample", bufs=2))
+        sum_pool = stack.enter_context(tc.psum_pool(name="sums", bufs=1))
+        turn_pool = stack.enter_context(tc.psum_pool(name="turn", bufs=4))
+
+        w_words = keep.tile([P, GROUPS, 2 * FEATS], U8, align_bytes=64)
+        w_planes = keep.tile([P, GROUPS, FEATS], U8, align_bytes=64)
+        identity = keep.tile([P, P], BF16)
+        w_occ_sb = keep.tile([P, P], BF16)
+        w_occ_t = keep.tile([P, P], BF16)
+        h_occ_sb = keep.tile([P, SAMPLES, VOXELS], BF16)
+        bias_rows = keep.tile([P, P], BF16)
+        bias_cols = keep.tile([P, FEAT_TILES], F32)
+        occ_grouped = keep.tile([P, SAMPLES, HALVES, MAPS, PACK], BF16, align_bytes=64)
+        occ_codes = keep.tile([P, SAMPLES, HALVES, MAPS], U32, align_bytes=64)
+        occ_planes = keep.tile([P, SAMPLES, HALVES, MAPS], U8, align_bytes=64)
+        result = keep.tile([P, SAMPLES, FEATS], F32)
+
+        nc.vector.memset(w_planes[:].rearrange("p g n -> p (g n)").bitcast(I32), 0)
+        nc.vector.memset(bias_rows[:], 0.0)
+        make_identity(nc, identity[:])
+        nc.sync.dma_start(out=w_occ_sb[:], in_=w_occ3)
+        nc.sync.dma_start(
+            out=bias_rows[0:FEAT_TILES, :], in_=b_add2.rearrange("(j c) -> j c", j=FEAT_TILES)
+        )
+        nc.sync.dma_start(out=h_occ_sb[:], in_=h_occ.rearrange("b c v -> c b v"))
+        scale_rows = w_add2_scales.rearrange("g (q r) n -> r q g n", r=PACK)
+        for r in range(PACK):
+            nc.sync.dma_start(
+                out=w_planes[r:P:32, :, :].bitcast(I32), in_=scale_rows[r].bitcast(I32)
+            )
+
+        def load_weight_words(first_group):
+            groups = slice(first_group, first_group + GROUPS // WEIGHT_LOADS)
+            nc.sync.dma_start(
+                out=w_words[:, groups, :].bitcast(I32),
+                in_=w_add2_words[groups].rearrange("g p w -> p g w").bitcast(I32),
+            )
+
+        bias_ps = turn_pool.tile([P, P], BF16, tag="turn")
+        nc.tensor.transpose(bias_ps[:], bias_rows[:], identity[:])
+        nc.vector.tensor_copy(out=bias_cols[:], in_=bias_ps[:, 0:FEAT_TILES])
+
+        w_occ_ps = turn_pool.tile([P, P], BF16, tag="turn")
+        nc.tensor.transpose(w_occ_ps[:], w_occ_sb[:], identity[:])
+        nc.vector.tensor_copy(out=w_occ_t[:], in_=w_occ_ps[:])
+        for b in range(SAMPLES):
+            for half in range(HALVES):
+                occ_ps = turn_pool.tile([P, PACK, MAPS], F32, tag="turn")
+                for t in range(PACK):
+                    nc.tensor.matmul(
+                        out=occ_ps[:, t, :],
+                        lhsT=h_occ_sb[:, b, half * K_PASS + t : (half + 1) * K_PASS : PACK],
+                        rhs=w_occ_t[:],
+                        start=True,
+                        stop=True,
+                    )
+                nc.scalar.activation(
+                    out=occ_grouped[:, b, half],
+                    in_=occ_ps[:].rearrange("p t o -> p o t"),
+                    func=ACT.Abs,
+                )
+
+        def load_and_regroup(b, g):
+            raw = raw_pool.tile([P, PACK, VOXELS], BF16)
+            nc.sync.dma_start(
+                out=raw[:],
+                in_=h_add[b, g * K_PASS : (g + 1) * K_PASS, :].rearrange("(p t) v -> p t v", t=PACK),
+            )
+            grouped = []
+            for half, copy in enumerate((nc.vector.tensor_copy, nc.scalar.copy)):
+                tile_half = chunk_pool.tile(
+                    [P, BANK, PACK], BF16, name="grouped%d" % half, align_bytes=64
+                )
+                copy(
+                    out=tile_half[:].rearrange("p (c i) t -> p c t i", i=RUN),
+                    in_=raw[:, :, half * BANK : (half + 1) * BANK].rearrange(
+                        "p t (c i) -> p c t i", i=RUN
+                    ),
+                )
+                grouped.append(tile_half)
+            return grouped
+
+        feat_sums = {}
+
+        def quantise_and_multiply(b, g, grouped):
+            if g == 0:
+                feat_sums[b] = [
+                    [
+                        sum_pool.tile([P, BANK], F32, name="sum%d%d" % (j, half))
+                        for half in range(HALVES)
+                    ]
+                    for j in range(FEAT_TILES)
+                ]
+            for half in range(HALVES):
+                codes = chunk_pool.tile([P, BANK], U32, name="codes%d" % half, align_bytes=64)
+                plane = chunk_pool.tile([P, BANK], U8, name="plane%d" % half, align_bytes=64)
+                nc.vector.quantize_mx(
+                    out=codes[:].bitcast(FP8X4),
+                    scales=plane[:],
+                    in_=grouped[half][:].rearrange("p v t -> p (v t)"),
+                )
+                for j in range(FEAT_TILES):
+                    nc.tensor.matmul_mx(
+                        out=feat_sums[b][j][half][:],
+                        lhsT=w_words[:, g, 2 * P * j : 2 * P * (j + 1)].bitcast(FP4X4),
+                        lhsT_scale=w_planes[:, g, P * j : P * (j + 1)],
+                        rhs=codes[:].bitcast(FP8X4),
+                        rhs_scale=plane[:],
+                        start=(g == 0),
+                        stop=(g == GROUPS - 1),
+                    )
+
+        feat_sorted = {}
+        feat_turned = {}
+        feat_grouped = {}
+        pooled = {}
+
+        def add_bias_and_transpose(b):
+            nc.vector.quantize_mx(
+                out=occ_codes[:, b].rearrange("p h o -> p (h o)").bitcast(FP8X4),
+                scales=occ_planes[:, b].rearrange("p h o -> p (h o)"),
+                in_=occ_grouped[:, b].rearrange("p h o t -> p (h o t)"),
+            )
+            feat_sorted[b] = sample_pool.tile(
+                [P, FEAT_TILES, HALVES, PACK, P], BF16, name="feat_sorted"
+            )
+            for half in range(HALVES):
+                nc.vector.tensor_scalar_add(
+                    out=feat_sorted[b][:, 0, half],
+                    in0=feat_sums[b][0][half][:].rearrange("c (p t) -> c t p", t=PACK),
+                    scalar1=bias_cols[:, 0:1],
+                )
+                nc.scalar.activation(
+                    out=feat_sorted[b][:, 1, half],
+                    in_=feat_sums[b][1][half][:].rearrange("c (p t) -> c t p", t=PACK),
+                    func=ACT.Identity,
+                    bias=bias_cols[:, 1:2],
+                )
+            feat_turned[b] = []
+            for half in range(HALVES):
+                banks = []
+                for j in range(FEAT_TILES):
+                    turned = turn_pool.tile([P, PACK, P], BF16, tag="turn", name="turned")
+                    for t in range(PACK):
+                        nc.tensor.transpose(
+                            turned[:, t, :], feat_sorted[b][:, j, half, t, :], identity[:]
+                        )
+                    banks.append(turned)
+                feat_turned[b].append(banks)
+
+        def regroup_feat(b):
+            feat_grouped[b] = sample_pool.tile(
+                [P, HALVES, FEATS, PACK], BF16, name="feat_grouped", align_bytes=64
+            )
+            for half in range(HALVES):
+                for j, copy in enumerate((nc.vector.tensor_copy, nc.scalar.copy)):
+                    copy(
+                        out=feat_grouped[b][:, half, P * j : P * (j + 1), :],
+                        in_=feat_turned[b][half][j][:].rearrange("p t c -> p c t"),
+                    )
+
+        def quantise_feat_and_multiply(b):
+            feat_codes = sample_pool.tile([P, HALVES, FEATS], U32, align_bytes=64)
+            feat_planes = sample_pool.tile([P, HALVES, FEATS], U8, align_bytes=64)
+            pooled[b] = turn_pool.tile([P, FEATS], F32, tag="turn", name="pooled")
+            for half in range(HALVES):
+                nc.vector.quantize_mx(
+                    out=feat_codes[:, half, :].bitcast(FP8X4),
+                    scales=feat_planes[:, half, :],
+                    in_=feat_grouped[b][:, half].rearrange("p c t -> p (c t)"),
+                )
+                nc.tensor.matmul_mx(
+                    out=pooled[b][:],
+                    lhsT=occ_codes[:, b, half, :].bitcast(FP8X4),
+                    lhsT_scale=occ_planes[:, b, half, :],
+                    rhs=feat_codes[:, half, :].bitcast(FP8X4),
+                    rhs_scale=feat_planes[:, half, :],
+                    start=(half == 0),
+                    stop=(half == HALVES - 1),
+                )
+
+        def take_mean(b):
+            nc.scalar.mul(out=result[:, b, :], in_=pooled[b][:], mul=1.0 / VOXELS)
+
+        pool_stages = (add_bias_and_transpose, regroup_feat, quantise_feat_and_multiply, take_mean)
+
+        waiting = None
+        for b in range(SAMPLES):
+            for g in range(GROUPS):
+                grouped = load_and_regroup(b, g)
+                if b == 0 and g % (GROUPS // WEIGHT_LOADS) == 0:
+                    load_weight_words(g)
+                if waiting is not None:
+                    quantise_and_multiply(*waiting)
+                if b > 0 and g < len(pool_stages):
+                    pool_stages[g](b - 1)
+                waiting = (b, g, grouped)
+        quantise_and_multiply(*waiting)
+        for b in range(SAMPLES - 1):
+            nc.sync.dma_start(out=out[b], in_=result[:, b, :])
+        for stage in pool_stages:
+            stage(SAMPLES - 1)
+        nc.sync.dma_start(out=out[SAMPLES - 1], in_=result[:, SAMPLES - 1, :])

@@ -28,6 +28,7 @@ FEAT_TILES = FEATS // P
 RUN = 4
 WEIGHT_LOADS = 4
 RAW_BUFS = 8
+CODE_BUFS = 6
 
 FLOPS = 2 * SAMPLES * VOXELS * (FEATS * CHANNELS + MAPS * P + MAPS * FEATS)
 
@@ -41,6 +42,7 @@ def tile_occurrencepool_pa_k_kernel(
         keep = stack.enter_context(tc.tile_pool(name="keep", bufs=1))
         raw_pool = stack.enter_context(tc.tile_pool(name="raw", bufs=RAW_BUFS))
         chunk_pool = stack.enter_context(tc.tile_pool(name="chunk", bufs=3))
+        codes_pool = stack.enter_context(tc.tile_pool(name="codes", bufs=CODE_BUFS))
         sample_pool = stack.enter_context(tc.tile_pool(name="sample", bufs=2))
         sum_pool = stack.enter_context(tc.psum_pool(name="sums", bufs=1))
         turn_pool = stack.enter_context(tc.psum_pool(name="turn", bufs=4))
@@ -66,11 +68,13 @@ def tile_occurrencepool_pa_k_kernel(
             out=bias_rows[0:FEAT_TILES, :], in_=b_add2.rearrange("(j c) -> j c", j=FEAT_TILES)
         )
         nc.sync.dma_start(out=h_occ_sb[:], in_=h_occ.rearrange("b c v -> c b v"))
-        scale_rows = w_add2_scales.rearrange("g (q r) n -> r q g n", r=PACK)
-        for r in range(PACK):
-            nc.sync.dma_start(
-                out=w_planes[r:P:32, :, :].bitcast(I32), in_=scale_rows[r].bitcast(I32)
-            )
+
+        def load_weight_scales():
+            scale_rows = w_add2_scales.rearrange("g (q r) n -> r q g n", r=PACK)
+            for r in range(PACK):
+                nc.sync.dma_start(
+                    out=w_planes[r:P:32, :, :].bitcast(I32), in_=scale_rows[r].bitcast(I32)
+                )
 
         def load_weight_words(first_group):
             groups = slice(first_group, first_group + GROUPS // WEIGHT_LOADS)
@@ -103,12 +107,18 @@ def tile_occurrencepool_pa_k_kernel(
                     func=ACT.Abs,
                 )
 
-        def load_and_regroup(b, g):
+        raw_chunks = {}
+
+        def load_chunk(b, g):
             raw = raw_pool.tile([P, PACK, VOXELS], BF16)
             nc.sync.dma_start(
                 out=raw[:],
                 in_=h_add[b, g * K_PASS : (g + 1) * K_PASS, :].rearrange("(p t) v -> p t v", t=PACK),
             )
+            raw_chunks[(b, g)] = raw
+
+        def regroup(b, g):
+            raw = raw_chunks[(b, g)]
             grouped = []
             for half, copy in enumerate((nc.vector.tensor_copy, nc.scalar.copy)):
                 tile_half = chunk_pool.tile(
@@ -135,8 +145,8 @@ def tile_occurrencepool_pa_k_kernel(
                     for j in range(FEAT_TILES)
                 ]
             for half in range(HALVES):
-                codes = chunk_pool.tile([P, BANK], U32, name="codes%d" % half, align_bytes=64)
-                plane = chunk_pool.tile([P, BANK], U8, name="plane%d" % half, align_bytes=64)
+                codes = codes_pool.tile([P, BANK], U32, name="codes%d" % half, align_bytes=64)
+                plane = codes_pool.tile([P, BANK], U8, name="plane%d" % half, align_bytes=64)
                 nc.vector.quantize_mx(
                     out=codes[:].bitcast(FP8X4),
                     scales=plane[:],
@@ -227,17 +237,22 @@ def tile_occurrencepool_pa_k_kernel(
 
         pool_stages = (add_bias_and_transpose, regroup_feat, quantise_feat_and_multiply, take_mean)
 
+        chunks = [(b, g) for b in range(SAMPLES) for g in range(GROUPS)]
         waiting = None
-        for b in range(SAMPLES):
-            for g in range(GROUPS):
-                grouped = load_and_regroup(b, g)
-                if b == 0 and g % (GROUPS // WEIGHT_LOADS) == 0:
-                    load_weight_words(g)
-                if waiting is not None:
-                    quantise_and_multiply(*waiting)
-                if b > 0 and g < len(pool_stages):
-                    pool_stages[g](b - 1)
-                waiting = (b, g, grouped)
+        load_chunk(*chunks[0])
+        for step, (b, g) in enumerate(chunks):
+            if step + 1 < len(chunks):
+                load_chunk(*chunks[step + 1])
+            if step == 0:
+                load_weight_scales()
+            if b == 0 and g % (GROUPS // WEIGHT_LOADS) == 0:
+                load_weight_words(g)
+            grouped = regroup(b, g)
+            if waiting is not None:
+                quantise_and_multiply(*waiting)
+            if b > 0 and g < len(pool_stages):
+                pool_stages[g](b - 1)
+            waiting = (b, g, grouped)
         quantise_and_multiply(*waiting)
         for b in range(SAMPLES - 1):
             nc.sync.dma_start(out=out[b], in_=result[:, b, :])

@@ -26,6 +26,7 @@ GROUPS = CHANNELS // K_PASS
 HALVES = VOXELS // BANK
 FEAT_TILES = FEATS // P
 RUN = 4
+VECTOR_VOXELS = 496
 WEIGHT_LOADS = 4
 RAW_BUFS = 8
 CODE_BUFS = 6
@@ -119,18 +120,16 @@ def tile_occurrencepool_pa_k_kernel(
 
         def regroup(b, g):
             raw = raw_chunks[(b, g)]
-            grouped = []
-            for half, copy in enumerate((nc.vector.tensor_copy, nc.scalar.copy)):
-                tile_half = chunk_pool.tile(
-                    [P, BANK, PACK], BF16, name="grouped%d" % half, align_bytes=64
-                )
+            grouped = chunk_pool.tile([P, VOXELS, PACK], BF16, align_bytes=64)
+            shares = (
+                (nc.vector.tensor_copy, slice(0, VECTOR_VOXELS)),
+                (nc.scalar.copy, slice(VECTOR_VOXELS, VOXELS)),
+            )
+            for copy, voxels in shares:
                 copy(
-                    out=tile_half[:].rearrange("p (c i) t -> p c t i", i=RUN),
-                    in_=raw[:, :, half * BANK : (half + 1) * BANK].rearrange(
-                        "p t (c i) -> p c t i", i=RUN
-                    ),
+                    out=grouped[:, voxels, :].rearrange("p (c i) t -> p c t i", i=RUN),
+                    in_=raw[:, :, voxels].rearrange("p t (c i) -> p c t i", i=RUN),
                 )
-                grouped.append(tile_half)
             return grouped
 
         feat_sums = {}
@@ -144,21 +143,25 @@ def tile_occurrencepool_pa_k_kernel(
                     ]
                     for j in range(FEAT_TILES)
                 ]
-            for half in range(HALVES):
-                codes = codes_pool.tile([P, BANK], U32, name="codes%d" % half, align_bytes=64)
-                plane = codes_pool.tile([P, BANK], U8, name="plane%d" % half, align_bytes=64)
+            codes = codes_pool.tile([P, VOXELS], U32, align_bytes=64)
+            plane = codes_pool.tile([P, VOXELS], U8, align_bytes=64)
+            pieces = HALVES if g == GROUPS - 1 else 1
+            for piece in range(pieces):
+                voxels = slice(piece * VOXELS // pieces, (piece + 1) * VOXELS // pieces)
                 nc.vector.quantize_mx(
-                    out=codes[:].bitcast(FP8X4),
-                    scales=plane[:],
-                    in_=grouped[half][:].rearrange("p v t -> p (v t)"),
+                    out=codes[:, voxels].bitcast(FP8X4),
+                    scales=plane[:, voxels],
+                    in_=grouped[:, voxels, :].rearrange("p v t -> p (v t)"),
                 )
+            for half in range(HALVES):
+                voxels = slice(half * BANK, (half + 1) * BANK)
                 for j in range(FEAT_TILES):
                     nc.tensor.matmul_mx(
                         out=feat_sums[b][j][half][:],
                         lhsT=w_words[:, g, 2 * P * j : 2 * P * (j + 1)].bitcast(FP4X4),
                         lhsT_scale=w_planes[:, g, P * j : P * (j + 1)],
-                        rhs=codes[:].bitcast(FP8X4),
-                        rhs_scale=plane[:],
+                        rhs=codes[:, voxels].bitcast(FP8X4),
+                        rhs_scale=plane[:, voxels],
                         start=(g == 0),
                         stop=(g == GROUPS - 1),
                     )

@@ -27,7 +27,9 @@ HALVES = VOXELS // BANK
 FEAT_TILES = FEATS // P
 RUN = 4
 VECTOR_VOXELS = 496
-WEIGHT_LOADS = 4
+WEIGHT_LOADS = 8
+OCC_LOAD_STEP = 4
+OCC_STEP = 8
 RAW_BUFS = 8
 CODE_BUFS = 6
 
@@ -64,11 +66,6 @@ def tile_occurrencepool_pa_k_kernel(
         nc.vector.memset(w_planes[:].rearrange("p g n -> p (g n)").bitcast(I32), 0)
         nc.vector.memset(bias_rows[:], 0.0)
         make_identity(nc, identity[:])
-        nc.sync.dma_start(out=w_occ_sb[:], in_=w_occ3)
-        nc.sync.dma_start(
-            out=bias_rows[0:FEAT_TILES, :], in_=b_add2.rearrange("(j c) -> j c", j=FEAT_TILES)
-        )
-        nc.sync.dma_start(out=h_occ_sb[:], in_=h_occ.rearrange("b c v -> c b v"))
 
         def load_weight_scales():
             scale_rows = w_add2_scales.rearrange("g (q r) n -> r q g n", r=PACK)
@@ -84,38 +81,48 @@ def tile_occurrencepool_pa_k_kernel(
                 in_=w_add2_words[groups].rearrange("g p w -> p g w").bitcast(I32),
             )
 
-        bias_ps = turn_pool.tile([P, P], BF16, tag="turn")
-        nc.tensor.transpose(bias_ps[:], bias_rows[:], identity[:])
-        nc.vector.tensor_copy(out=bias_cols[:], in_=bias_ps[:, 0:FEAT_TILES])
+        def load_small_weights():
+            nc.sync.dma_start(out=w_occ_sb[:], in_=w_occ3)
+            nc.sync.dma_start(
+                out=bias_rows[0:FEAT_TILES, :], in_=b_add2.rearrange("(j c) -> j c", j=FEAT_TILES)
+            )
 
-        w_occ_ps = turn_pool.tile([P, P], BF16, tag="turn")
-        nc.tensor.transpose(w_occ_ps[:], w_occ_sb[:], identity[:])
-        nc.vector.tensor_copy(out=w_occ_t[:], in_=w_occ_ps[:])
-        for b in range(SAMPLES):
-            for half in range(HALVES):
-                occ_ps = turn_pool.tile([P, PACK, MAPS], F32, tag="turn")
-                for t in range(PACK):
-                    nc.tensor.matmul(
-                        out=occ_ps[:, t, :],
-                        lhsT=h_occ_sb[:, b, half * K_PASS + t : (half + 1) * K_PASS : PACK],
-                        rhs=w_occ_t[:],
-                        start=True,
-                        stop=True,
-                    )
-                nc.scalar.activation(
-                    out=occ_grouped[:, b, half],
-                    in_=occ_ps[:].rearrange("p t o -> p o t"),
-                    func=ACT.Abs,
+        def turn_small_weights():
+            bias_ps = turn_pool.tile([P, P], BF16, tag="turn", name="bias_ps")
+            nc.tensor.transpose(bias_ps[:], bias_rows[:], identity[:])
+            nc.vector.tensor_copy(out=bias_cols[:], in_=bias_ps[:, 0:FEAT_TILES])
+            w_occ_ps = turn_pool.tile([P, P], BF16, tag="turn", name="w_occ_ps")
+            nc.tensor.transpose(w_occ_ps[:], w_occ_sb[:], identity[:])
+            nc.vector.tensor_copy(out=w_occ_t[:], in_=w_occ_ps[:])
+
+        def make_occ(b, half):
+            occ_ps = turn_pool.tile([P, PACK, MAPS], F32, tag="turn", name="occ_ps")
+            for t in range(PACK):
+                nc.tensor.matmul(
+                    out=occ_ps[:, t, :],
+                    lhsT=h_occ_sb[:, b, half * K_PASS + t : (half + 1) * K_PASS : PACK],
+                    rhs=w_occ_t[:],
+                    start=True,
+                    stop=True,
                 )
+            nc.scalar.activation(
+                out=occ_grouped[:, b, half],
+                in_=occ_ps[:].rearrange("p t o -> p o t"),
+                func=ACT.Abs,
+            )
 
         raw_chunks = {}
 
         def load_chunk(b, g):
             raw = raw_pool.tile([P, PACK, VOXELS], BF16)
-            nc.sync.dma_start(
-                out=raw[:],
-                in_=h_add[b, g * K_PASS : (g + 1) * K_PASS, :].rearrange("(p t) v -> p t v", t=PACK),
+            rows = h_add[b, g * K_PASS : (g + 1) * K_PASS, :].rearrange("(p t) v -> p t v", t=PACK)
+            cuts = (
+                (slice(VECTOR_VOXELS, VOXELS), slice(0, VECTOR_VOXELS))
+                if (b, g) == (0, 0)
+                else (slice(0, VOXELS),)
             )
+            for voxels in cuts:
+                nc.sync.dma_start(out=raw[:, :, voxels], in_=rows[:, :, voxels])
             raw_chunks[(b, g)] = raw
 
         def regroup(b, g):
@@ -250,9 +257,17 @@ def tile_occurrencepool_pa_k_kernel(
                 load_weight_scales()
             if b == 0 and g % (GROUPS // WEIGHT_LOADS) == 0:
                 load_weight_words(g)
+            if g == OCC_LOAD_STEP:
+                if b == 0:
+                    load_small_weights()
+                nc.sync.dma_start(out=h_occ_sb[:, b, :], in_=h_occ[b])
             grouped = regroup(b, g)
             if waiting is not None:
                 quantise_and_multiply(*waiting)
+            if b == 0 and g == OCC_STEP:
+                turn_small_weights()
+            if OCC_STEP <= g < OCC_STEP + HALVES:
+                make_occ(b, g - OCC_STEP)
             if b > 0 and g < len(pool_stages):
                 pool_stages[g](b - 1)
             waiting = (b, g, grouped)

@@ -62,7 +62,11 @@ def tile_occurrencepool_pa_k_kernel(
         occ_codes = keep.tile([P, SAMPLES, HALVES, MAPS], U32, align_bytes=64)
         occ_planes = keep.tile([P, SAMPLES, HALVES, MAPS], U8, align_bytes=64)
         result = keep.tile([P, SAMPLES, FEATS], F32)
+        warm = keep.tile([P, 1], F32)
+        warm_out = keep.tile([P, 1], F32)
 
+        nc.gpsimd.memset(warm[:], 0.0)
+        nc.scalar.activation(out=warm_out[:], in_=warm[:], func=ACT.Abs)
         nc.vector.memset(w_planes[:].rearrange("p g n -> p (g n)").bitcast(I32), 0)
         nc.vector.memset(bias_rows[:], 0.0)
         make_identity(nc, identity[:])
@@ -87,15 +91,43 @@ def tile_occurrencepool_pa_k_kernel(
                 out=bias_rows[0:FEAT_TILES, :], in_=b_add2.rearrange("(j c) -> j c", j=FEAT_TILES)
             )
 
+        turned_weights = []
+
         def turn_small_weights():
-            bias_ps = turn_pool.tile([P, P], BF16, tag="turn", name="bias_ps")
-            nc.tensor.transpose(bias_ps[:], bias_rows[:], identity[:])
+            for rows in (bias_rows, w_occ_sb):
+                turned = turn_pool.tile([P, P], BF16, tag="turn", name="turned_weight")
+                nc.tensor.transpose(turned[:], rows[:], identity[:])
+                turned_weights.append(turned)
+
+        def copy_small_weights():
+            bias_ps, w_occ_ps = turned_weights
             nc.vector.tensor_copy(out=bias_cols[:], in_=bias_ps[:, 0:FEAT_TILES])
-            w_occ_ps = turn_pool.tile([P, P], BF16, tag="turn", name="w_occ_ps")
-            nc.tensor.transpose(w_occ_ps[:], w_occ_sb[:], identity[:])
             nc.vector.tensor_copy(out=w_occ_t[:], in_=w_occ_ps[:])
 
-        def make_occ(b, half):
+        def quantise_occ(b):
+            nc.vector.quantize_mx(
+                out=occ_codes[:, b].rearrange("p h o -> p (h o)").bitcast(FP8X4),
+                scales=occ_planes[:, b].rearrange("p h o -> p (h o)"),
+                in_=occ_grouped[:, b].rearrange("p h o t -> p (h o t)"),
+            )
+
+        def occ_step(b, step):
+            first = OCC_STEP if b > 0 else OCC_STEP + 2
+            if step == OCC_STEP and b == 0:
+                turn_small_weights()
+            if step == OCC_STEP + 1 and b == 0:
+                copy_small_weights()
+            for half in range(HALVES):
+                if step == first + half:
+                    multiply_occ(b, half)
+                if step == first + half + 1:
+                    take_abs(b, half)
+            if step == first + HALVES + 1:
+                quantise_occ(b)
+
+        occ_sums = {}
+
+        def multiply_occ(b, half):
             occ_ps = turn_pool.tile([P, PACK, MAPS], F32, tag="turn", name="occ_ps")
             for t in range(PACK):
                 nc.tensor.matmul(
@@ -105,9 +137,12 @@ def tile_occurrencepool_pa_k_kernel(
                     start=True,
                     stop=True,
                 )
+            occ_sums[(b, half)] = occ_ps
+
+        def take_abs(b, half):
             nc.scalar.activation(
                 out=occ_grouped[:, b, half],
-                in_=occ_ps[:].rearrange("p t o -> p o t"),
+                in_=occ_sums[(b, half)][:].rearrange("p t o -> p o t"),
                 func=ACT.Abs,
             )
 
@@ -176,68 +211,70 @@ def tile_occurrencepool_pa_k_kernel(
         feat_sorted = {}
         feat_turned = {}
         feat_grouped = {}
+        feat_quantised = {}
         pooled = {}
 
-        def add_bias_and_transpose(b):
-            nc.vector.quantize_mx(
-                out=occ_codes[:, b].rearrange("p h o -> p (h o)").bitcast(FP8X4),
-                scales=occ_planes[:, b].rearrange("p h o -> p (h o)"),
-                in_=occ_grouped[:, b].rearrange("p h o t -> p (h o t)"),
-            )
-            feat_sorted[b] = sample_pool.tile(
-                [P, FEAT_TILES, HALVES, PACK, P], BF16, name="feat_sorted"
-            )
-            for half in range(HALVES):
-                nc.vector.tensor_scalar_add(
-                    out=feat_sorted[b][:, 0, half],
-                    in0=feat_sums[b][0][half][:].rearrange("c (p t) -> c t p", t=PACK),
-                    scalar1=bias_cols[:, 0:1],
+        def add_bias(b, half):
+            if half == 0:
+                feat_sorted[b] = sample_pool.tile(
+                    [P, FEAT_TILES, HALVES, PACK, P], BF16, name="feat_sorted"
                 )
-                nc.scalar.activation(
-                    out=feat_sorted[b][:, 1, half],
-                    in_=feat_sums[b][1][half][:].rearrange("c (p t) -> c t p", t=PACK),
-                    func=ACT.Identity,
-                    bias=bias_cols[:, 1:2],
-                )
-            feat_turned[b] = []
-            for half in range(HALVES):
-                banks = []
-                for j in range(FEAT_TILES):
-                    turned = turn_pool.tile([P, PACK, P], BF16, tag="turn", name="turned")
-                    for t in range(PACK):
-                        nc.tensor.transpose(
-                            turned[:, t, :], feat_sorted[b][:, j, half, t, :], identity[:]
-                        )
-                    banks.append(turned)
-                feat_turned[b].append(banks)
+            nc.vector.tensor_scalar_add(
+                out=feat_sorted[b][:, 0, half],
+                in0=feat_sums[b][0][half][:].rearrange("c (p t) -> c t p", t=PACK),
+                scalar1=bias_cols[:, 0:1],
+            )
+            nc.scalar.activation(
+                out=feat_sorted[b][:, 1, half],
+                in_=feat_sums[b][1][half][:].rearrange("c (p t) -> c t p", t=PACK),
+                func=ACT.Identity,
+                bias=bias_cols[:, 1:2],
+            )
 
-        def regroup_feat(b):
-            feat_grouped[b] = sample_pool.tile(
-                [P, HALVES, FEATS, PACK], BF16, name="feat_grouped", align_bytes=64
-            )
-            for half in range(HALVES):
-                for j, copy in enumerate((nc.vector.tensor_copy, nc.scalar.copy)):
-                    copy(
-                        out=feat_grouped[b][:, half, P * j : P * (j + 1), :],
-                        in_=feat_turned[b][half][j][:].rearrange("p t c -> p c t"),
+        def transpose_feat(b, half):
+            banks = []
+            for j in range(FEAT_TILES):
+                turned = turn_pool.tile([P, PACK, P], BF16, tag="turn", name="turned")
+                for t in range(PACK):
+                    nc.tensor.transpose(
+                        turned[:, t, :], feat_sorted[b][:, j, half, t, :], identity[:]
                     )
+                banks.append(turned)
+            feat_turned[(b, half)] = banks
 
-        def quantise_feat_and_multiply(b):
-            feat_codes = sample_pool.tile([P, HALVES, FEATS], U32, align_bytes=64)
-            feat_planes = sample_pool.tile([P, HALVES, FEATS], U8, align_bytes=64)
+        def regroup_feat(b, half):
+            if half == 0:
+                feat_grouped[b] = sample_pool.tile(
+                    [P, HALVES, FEATS, PACK], BF16, name="feat_grouped", align_bytes=64
+                )
+            for j, copy in enumerate((nc.vector.tensor_copy, nc.scalar.copy)):
+                copy(
+                    out=feat_grouped[b][:, half, P * j : P * (j + 1), :],
+                    in_=feat_turned[(b, half)][j][:].rearrange("p t c -> p c t"),
+                )
+
+        def quantise_feat(b, half):
+            if half == 0:
+                feat_codes = sample_pool.tile([P, HALVES, FEATS], U32, align_bytes=64)
+                feat_planes = sample_pool.tile([P, HALVES, FEATS], U8, align_bytes=64)
+                feat_quantised[b] = (feat_codes, feat_planes)
+            codes, planes = feat_quantised[b]
+            nc.vector.quantize_mx(
+                out=codes[:, half, :].bitcast(FP8X4),
+                scales=planes[:, half, :],
+                in_=feat_grouped[b][:, half].rearrange("p c t -> p (c t)"),
+            )
+
+        def multiply_feat(b):
+            codes, planes = feat_quantised[b]
             pooled[b] = turn_pool.tile([P, FEATS], F32, tag="turn", name="pooled")
             for half in range(HALVES):
-                nc.vector.quantize_mx(
-                    out=feat_codes[:, half, :].bitcast(FP8X4),
-                    scales=feat_planes[:, half, :],
-                    in_=feat_grouped[b][:, half].rearrange("p c t -> p (c t)"),
-                )
                 nc.tensor.matmul_mx(
                     out=pooled[b][:],
                     lhsT=occ_codes[:, b, half, :].bitcast(FP8X4),
                     lhsT_scale=occ_planes[:, b, half, :],
-                    rhs=feat_codes[:, half, :].bitcast(FP8X4),
-                    rhs_scale=feat_planes[:, half, :],
+                    rhs=codes[:, half, :].bitcast(FP8X4),
+                    rhs_scale=planes[:, half, :],
                     start=(half == 0),
                     stop=(half == HALVES - 1),
                 )
@@ -245,7 +282,22 @@ def tile_occurrencepool_pa_k_kernel(
         def take_mean(b):
             nc.scalar.mul(out=result[:, b, :], in_=pooled[b][:], mul=1.0 / VOXELS)
 
-        pool_stages = (add_bias_and_transpose, regroup_feat, quantise_feat_and_multiply, take_mean)
+        def pool_step(b, step):
+            if step == 1:
+                add_bias(b, 0)
+                add_bias(b, 1)
+                transpose_feat(b, 0)
+            elif step == 2:
+                regroup_feat(b, 0)
+                transpose_feat(b, 1)
+            elif step == 3:
+                quantise_feat(b, 0)
+                regroup_feat(b, 1)
+            elif step == 4:
+                quantise_feat(b, 1)
+                multiply_feat(b)
+            elif step == 5:
+                take_mean(b)
 
         chunks = [(b, g) for b in range(SAMPLES) for g in range(GROUPS)]
         waiting = None
@@ -262,18 +314,23 @@ def tile_occurrencepool_pa_k_kernel(
                     load_small_weights()
                 nc.sync.dma_start(out=h_occ_sb[:, b, :], in_=h_occ[b])
             grouped = regroup(b, g)
+            occ_step(b, g)
+            if b > 0:
+                pool_step(b - 1, g)
             if waiting is not None:
                 quantise_and_multiply(*waiting)
-            if b == 0 and g == OCC_STEP:
-                turn_small_weights()
-            if OCC_STEP <= g < OCC_STEP + HALVES:
-                make_occ(b, g - OCC_STEP)
-            if b > 0 and g < len(pool_stages):
-                pool_stages[g](b - 1)
             waiting = (b, g, grouped)
         quantise_and_multiply(*waiting)
         for b in range(SAMPLES - 1):
             nc.sync.dma_start(out=out[b], in_=result[:, b, :])
-        for stage in pool_stages:
-            stage(SAMPLES - 1)
+        last = SAMPLES - 1
+        for half in range(HALVES):
+            add_bias(last, half)
+            transpose_feat(last, half)
+        for half in range(HALVES):
+            regroup_feat(last, half)
+        for half in range(HALVES):
+            quantise_feat(last, half)
+        multiply_feat(last)
+        take_mean(last)
         nc.sync.dma_start(out=out[SAMPLES - 1], in_=result[:, SAMPLES - 1, :])

@@ -26,7 +26,11 @@ GROUPS = CHANNELS // K_PASS
 HALVES = VOXELS // BANK
 FEAT_TILES = FEATS // P
 RUN = 4
-VECTOR_VOXELS = 496
+VECTOR_VOXELS = 448
+SCALAR_VOXELS = 384
+TENSOR_FIRST = VECTOR_VOXELS + SCALAR_VOXELS
+TENSOR_VOXELS = VOXELS - TENSOR_FIRST
+TENSOR_PIECES = 2
 WEIGHT_LOADS = 8
 OCC_LOAD_STEP = 4
 OCC_STEP = 8
@@ -48,7 +52,8 @@ def tile_occurrencepool_pa_k_kernel(
         codes_pool = stack.enter_context(tc.tile_pool(name="codes", bufs=CODE_BUFS))
         sample_pool = stack.enter_context(tc.tile_pool(name="sample", bufs=2))
         sum_pool = stack.enter_context(tc.psum_pool(name="sums", bufs=1))
-        turn_pool = stack.enter_context(tc.psum_pool(name="turn", bufs=4))
+        turn_pool = stack.enter_context(tc.psum_pool(name="turn", bufs=2))
+        inter_pool = stack.enter_context(tc.psum_pool(name="inter", bufs=2))
 
         w_words = keep.tile([P, GROUPS, 2 * FEATS], U8, align_bytes=64)
         w_planes = keep.tile([P, GROUPS, FEATS], U8, align_bytes=64)
@@ -160,18 +165,36 @@ def tile_occurrencepool_pa_k_kernel(
                 nc.sync.dma_start(out=raw[:, :, voxels], in_=rows[:, :, voxels])
             raw_chunks[(b, g)] = raw
 
+        inter_chunks = {}
+
+        def regroup_on_tensor(b, g):
+            raw = raw_chunks[(b, g)]
+            inter = inter_pool.tile([P, TENSOR_VOXELS, PACK], BF16, tag="inter", name="inter")
+            width = TENSOR_VOXELS // TENSOR_PIECES
+            for piece in range(TENSOR_PIECES):
+                first = piece * width
+                nc.tensor.matmul(
+                    out=inter[:, first : first + width, :].rearrange("p v t -> p t v"),
+                    lhsT=identity[:],
+                    rhs=raw[:, :, TENSOR_FIRST + first : TENSOR_FIRST + first + width],
+                    start=True,
+                    stop=True,
+                )
+            inter_chunks[(b, g)] = inter
+
         def regroup(b, g):
             raw = raw_chunks[(b, g)]
             grouped = chunk_pool.tile([P, VOXELS, PACK], BF16, align_bytes=64)
             shares = (
                 (nc.vector.tensor_copy, slice(0, VECTOR_VOXELS)),
-                (nc.scalar.copy, slice(VECTOR_VOXELS, VOXELS)),
+                (nc.scalar.copy, slice(VECTOR_VOXELS, VECTOR_VOXELS + SCALAR_VOXELS)),
             )
             for copy, voxels in shares:
                 copy(
                     out=grouped[:, voxels, :].rearrange("p (c i) t -> p c t i", i=RUN),
                     in_=raw[:, :, voxels].rearrange("p t (c i) -> p c t i", i=RUN),
                 )
+            nc.scalar.copy(out=grouped[:, TENSOR_FIRST:VOXELS, :], in_=inter_chunks[(b, g)][:])
             return grouped
 
         feat_sums = {}
@@ -234,7 +257,10 @@ def tile_occurrencepool_pa_k_kernel(
         def transpose_feat(b, half):
             banks = []
             for j in range(FEAT_TILES):
-                turned = turn_pool.tile([P, PACK, P], BF16, tag="turn", name="turned")
+                if (b, half) == (SAMPLES - 1, HALVES - 1):
+                    turned = inter_pool.tile([P, PACK, P], BF16, tag="inter", name="turned")
+                else:
+                    turned = turn_pool.tile([P, PACK, P], BF16, tag="turn", name="turned")
                 for t in range(PACK):
                     nc.tensor.transpose(
                         turned[:, t, :], feat_sorted[b][:, j, half, t, :], identity[:]
@@ -302,9 +328,9 @@ def tile_occurrencepool_pa_k_kernel(
         chunks = [(b, g) for b in range(SAMPLES) for g in range(GROUPS)]
         waiting = None
         load_chunk(*chunks[0])
+        load_chunk(*chunks[1])
+        regroup_on_tensor(*chunks[0])
         for step, (b, g) in enumerate(chunks):
-            if step + 1 < len(chunks):
-                load_chunk(*chunks[step + 1])
             if step == 0:
                 load_weight_scales()
             if b == 0 and g % (GROUPS // WEIGHT_LOADS) == 0:
@@ -313,6 +339,10 @@ def tile_occurrencepool_pa_k_kernel(
                 if b == 0:
                     load_small_weights()
                 nc.sync.dma_start(out=h_occ_sb[:, b, :], in_=h_occ[b])
+            if step + 2 < len(chunks):
+                load_chunk(*chunks[step + 2])
+            if step + 1 < len(chunks):
+                regroup_on_tensor(*chunks[step + 1])
             grouped = regroup(b, g)
             occ_step(b, g)
             if b > 0:

@@ -174,9 +174,11 @@ def tile_occurrencepool_pa_k_kernel(
             for piece in range(TENSOR_PIECES):
                 first = piece * width
                 nc.tensor.matmul(
-                    out=inter[:, first : first + width, :].rearrange("p v t -> p t v"),
+                    out=inter[:, first : first + width, :],
                     lhsT=identity[:],
-                    rhs=raw[:, :, TENSOR_FIRST + first : TENSOR_FIRST + first + width],
+                    rhs=raw[:, :, TENSOR_FIRST + first : TENSOR_FIRST + first + width].rearrange(
+                        "p t v -> p v t"
+                    ),
                     start=True,
                     stop=True,
                 )

@@ -26,11 +26,9 @@ GROUPS = CHANNELS // K_PASS
 HALVES = VOXELS // BANK
 FEAT_TILES = FEATS // P
 RUN = 4
-VECTOR_VOXELS = 448
-SCALAR_VOXELS = 384
-TENSOR_FIRST = VECTOR_VOXELS + SCALAR_VOXELS
-TENSOR_VOXELS = VOXELS - TENSOR_FIRST
-TENSOR_PIECES = 2
+VECTOR_VOXELS = (464, 416)
+SCALAR_VOXELS = (432, 352)
+TENSOR_PIECE = BANK // PACK
 WEIGHT_LOADS = 8
 OCC_LOAD_STEP = 4
 OCC_STEP = 8
@@ -58,6 +56,7 @@ def tile_occurrencepool_pa_k_kernel(
         w_words = keep.tile([P, GROUPS, 2 * FEATS], U8, align_bytes=64)
         w_planes = keep.tile([P, GROUPS, FEATS], U8, align_bytes=64)
         identity = keep.tile([P, P], BF16)
+        word_identity = keep.tile([P, P], F32)
         w_occ_sb = keep.tile([P, P], BF16)
         w_occ_t = keep.tile([P, P], BF16)
         h_occ_sb = keep.tile([P, SAMPLES, VOXELS], BF16)
@@ -75,6 +74,7 @@ def tile_occurrencepool_pa_k_kernel(
         nc.vector.memset(w_planes[:].rearrange("p g n -> p (g n)").bitcast(I32), 0)
         nc.vector.memset(bias_rows[:], 0.0)
         make_identity(nc, identity[:])
+        make_identity(nc, word_identity[:])
 
         def load_weight_scales():
             scale_rows = w_add2_scales.rearrange("g (q r) n -> r q g n", r=PACK)
@@ -127,7 +127,7 @@ def tile_occurrencepool_pa_k_kernel(
                     multiply_occ(b, half)
                 if step == first + half + 1:
                     take_abs(b, half)
-            if step == first + HALVES + 1:
+            if step == first + HALVES + 2:
                 quantise_occ(b)
 
         occ_sums = {}
@@ -157,7 +157,7 @@ def tile_occurrencepool_pa_k_kernel(
             raw = raw_pool.tile([P, PACK, VOXELS], BF16)
             rows = h_add[b, g * K_PASS : (g + 1) * K_PASS, :].rearrange("(p t) v -> p t v", t=PACK)
             cuts = (
-                (slice(VECTOR_VOXELS, VOXELS), slice(0, VECTOR_VOXELS))
+                (slice(VECTOR_VOXELS[b], VOXELS), slice(0, VECTOR_VOXELS[b]))
                 if (b, g) == (0, 0)
                 else (slice(0, VOXELS),)
             )
@@ -169,14 +169,13 @@ def tile_occurrencepool_pa_k_kernel(
 
         def regroup_on_tensor(b, g):
             raw = raw_chunks[(b, g)]
-            inter = inter_pool.tile([P, TENSOR_VOXELS, PACK], BF16, tag="inter", name="inter")
-            width = TENSOR_VOXELS // TENSOR_PIECES
-            for piece in range(TENSOR_PIECES):
-                first = piece * width
+            first = VECTOR_VOXELS[b] + SCALAR_VOXELS[b]
+            inter = inter_pool.tile([P, VOXELS - first, PACK], BF16, tag="inter", name="inter")
+            for start in range(0, VOXELS - first, TENSOR_PIECE):
                 nc.tensor.matmul(
-                    out=inter[:, first : first + width, :],
+                    out=inter[:, start : start + TENSOR_PIECE, :],
                     lhsT=identity[:],
-                    rhs=raw[:, :, TENSOR_FIRST + first : TENSOR_FIRST + first + width].rearrange(
+                    rhs=raw[:, :, first + start : first + start + TENSOR_PIECE].rearrange(
                         "p t v -> p v t"
                     ),
                     start=True,
@@ -187,16 +186,17 @@ def tile_occurrencepool_pa_k_kernel(
         def regroup(b, g):
             raw = raw_chunks[(b, g)]
             grouped = chunk_pool.tile([P, VOXELS, PACK], BF16, align_bytes=64)
+            scalar_end = VECTOR_VOXELS[b] + SCALAR_VOXELS[b]
             shares = (
-                (nc.vector.tensor_copy, slice(0, VECTOR_VOXELS)),
-                (nc.scalar.copy, slice(VECTOR_VOXELS, VECTOR_VOXELS + SCALAR_VOXELS)),
+                (nc.vector.tensor_copy, slice(0, VECTOR_VOXELS[b])),
+                (nc.scalar.copy, slice(VECTOR_VOXELS[b], scalar_end)),
             )
             for copy, voxels in shares:
                 copy(
                     out=grouped[:, voxels, :].rearrange("p (c i) t -> p c t i", i=RUN),
                     in_=raw[:, :, voxels].rearrange("p t (c i) -> p c t i", i=RUN),
                 )
-            nc.scalar.copy(out=grouped[:, TENSOR_FIRST:VOXELS, :], in_=inter_chunks[(b, g)][:])
+            nc.scalar.copy(out=grouped[:, scalar_end:VOXELS, :], in_=inter_chunks[(b, g)][:])
             return grouped
 
         feat_sums = {}
@@ -212,7 +212,7 @@ def tile_occurrencepool_pa_k_kernel(
                 ]
             codes = codes_pool.tile([P, VOXELS], U32, align_bytes=64)
             plane = codes_pool.tile([P, VOXELS], U8, align_bytes=64)
-            pieces = HALVES if g == GROUPS - 1 else 1
+            pieces = HALVES if g == GROUPS - 1 or (b, g) == (SAMPLES - 1, GROUPS - 2) else 1
             for piece in range(pieces):
                 voxels = slice(piece * VOXELS // pieces, (piece + 1) * VOXELS // pieces)
                 nc.vector.quantize_mx(
@@ -233,7 +233,7 @@ def tile_occurrencepool_pa_k_kernel(
                         stop=(g == GROUPS - 1),
                     )
 
-        feat_sorted = {}
+        feat_rounded = {}
         feat_turned = {}
         feat_grouped = {}
         feat_quantised = {}
@@ -241,32 +241,31 @@ def tile_occurrencepool_pa_k_kernel(
 
         def add_bias(b, half):
             if half == 0:
-                feat_sorted[b] = sample_pool.tile(
-                    [P, FEAT_TILES, HALVES, PACK, P], BF16, name="feat_sorted"
-                )
+                feat_rounded[b] = sample_pool.tile([P, FEAT_TILES, VOXELS], BF16, name="feat_rounded")
+            voxels = slice(half * BANK, (half + 1) * BANK)
             nc.vector.tensor_scalar_add(
-                out=feat_sorted[b][:, 0, half],
-                in0=feat_sums[b][0][half][:].rearrange("c (p t) -> c t p", t=PACK),
+                out=feat_rounded[b][:, 0, voxels],
+                in0=feat_sums[b][0][half][:],
                 scalar1=bias_cols[:, 0:1],
             )
             nc.scalar.activation(
-                out=feat_sorted[b][:, 1, half],
-                in_=feat_sums[b][1][half][:].rearrange("c (p t) -> c t p", t=PACK),
+                out=feat_rounded[b][:, 1, voxels],
+                in_=feat_sums[b][1][half][:],
                 func=ACT.Identity,
                 bias=bias_cols[:, 1:2],
             )
 
         def transpose_feat(b, half):
+            voxels = slice(half * BANK, (half + 1) * BANK)
             banks = []
             for j in range(FEAT_TILES):
                 if (b, half) == (SAMPLES - 1, HALVES - 1):
-                    turned = inter_pool.tile([P, PACK, P], BF16, tag="inter", name="turned")
+                    turned = inter_pool.tile([P, 2, P], F32, tag="inter", name="turned")
                 else:
-                    turned = turn_pool.tile([P, PACK, P], BF16, tag="turn", name="turned")
-                for t in range(PACK):
-                    nc.tensor.transpose(
-                        turned[:, t, :], feat_sorted[b][:, j, half, t, :], identity[:]
-                    )
+                    turned = turn_pool.tile([P, 2, P], F32, tag="turn", name="turned")
+                words = feat_rounded[b][:, j, voxels].bitcast(F32)
+                for u in range(2):
+                    nc.tensor.transpose(turned[:, u, :], words[:, u::2], word_identity[:])
                 banks.append(turned)
             feat_turned[(b, half)] = banks
 
@@ -277,20 +276,18 @@ def tile_occurrencepool_pa_k_kernel(
                 )
             for j, copy in enumerate((nc.vector.tensor_copy, nc.scalar.copy)):
                 copy(
-                    out=feat_grouped[b][:, half, P * j : P * (j + 1), :],
-                    in_=feat_turned[(b, half)][j][:].rearrange("p t c -> p c t"),
+                    out=feat_grouped[b][:, half, P * j : P * (j + 1), :].bitcast(F32),
+                    in_=feat_turned[(b, half)][j][:].rearrange("p u c -> p c u"),
                 )
 
-        def quantise_feat(b, half):
-            if half == 0:
-                feat_codes = sample_pool.tile([P, HALVES, FEATS], U32, align_bytes=64)
-                feat_planes = sample_pool.tile([P, HALVES, FEATS], U8, align_bytes=64)
-                feat_quantised[b] = (feat_codes, feat_planes)
-            codes, planes = feat_quantised[b]
+        def quantise_feat(b):
+            feat_codes = sample_pool.tile([P, HALVES, FEATS], U32, align_bytes=64)
+            feat_planes = sample_pool.tile([P, HALVES, FEATS], U8, align_bytes=64)
+            feat_quantised[b] = (feat_codes, feat_planes)
             nc.vector.quantize_mx(
-                out=codes[:, half, :].bitcast(FP8X4),
-                scales=planes[:, half, :],
-                in_=feat_grouped[b][:, half].rearrange("p c t -> p (c t)"),
+                out=feat_codes[:].rearrange("p h c -> p (h c)").bitcast(FP8X4),
+                scales=feat_planes[:].rearrange("p h c -> p (h c)"),
+                in_=feat_grouped[b][:].rearrange("p h c t -> p (h c t)"),
             )
 
         def multiply_feat(b):
@@ -319,10 +316,9 @@ def tile_occurrencepool_pa_k_kernel(
                 regroup_feat(b, 0)
                 transpose_feat(b, 1)
             elif step == 3:
-                quantise_feat(b, 0)
                 regroup_feat(b, 1)
             elif step == 4:
-                quantise_feat(b, 1)
+                quantise_feat(b)
                 multiply_feat(b)
             elif step == 5:
                 take_mean(b)
@@ -361,8 +357,7 @@ def tile_occurrencepool_pa_k_kernel(
             transpose_feat(last, half)
         for half in range(HALVES):
             regroup_feat(last, half)
-        for half in range(HALVES):
-            quantise_feat(last, half)
+        quantise_feat(last)
         multiply_feat(last)
         take_mean(last)
         nc.sync.dma_start(out=out[SAMPLES - 1], in_=result[:, SAMPLES - 1, :])

@@ -28,7 +28,7 @@ FEAT_TILES = FEATS // P
 RUN = 4
 VECTOR_VOXELS = (464, 416)
 SCALAR_VOXELS = (432, 352)
-TENSOR_PIECE = BANK // PACK
+TENSOR_PIECE = 128
 WEIGHT_LOADS = 8
 OCC_LOAD_STEP = 4
 OCC_STEP = 8
@@ -172,15 +172,17 @@ def tile_occurrencepool_pa_k_kernel(
             first = VECTOR_VOXELS[b] + SCALAR_VOXELS[b]
             inter = inter_pool.tile([P, VOXELS - first, PACK], BF16, tag="inter", name="inter")
             for start in range(0, VOXELS - first, TENSOR_PIECE):
-                nc.tensor.matmul(
-                    out=inter[:, start : start + TENSOR_PIECE, :],
-                    lhsT=identity[:],
-                    rhs=raw[:, :, first + start : first + start + TENSOR_PIECE].rearrange(
-                        "p t v -> p v t"
-                    ),
-                    start=True,
-                    stop=True,
-                )
+                voxels = slice(start, start + TENSOR_PIECE)
+                for t in range(0, PACK, 2):
+                    nc.tensor.matmul(
+                        out=inter[:, voxels, t : t + 2],
+                        lhsT=identity[:],
+                        rhs=raw[:, t : t + 2, first + voxels.start : first + voxels.stop].rearrange(
+                            "p t v -> p v t"
+                        ),
+                        start=True,
+                        stop=True,
+                    )
             inter_chunks[(b, g)] = inter
 
         def regroup(b, g):
@@ -280,14 +282,16 @@ def tile_occurrencepool_pa_k_kernel(
                     in_=feat_turned[(b, half)][j][:].rearrange("p u c -> p c u"),
                 )
 
-        def quantise_feat(b):
-            feat_codes = sample_pool.tile([P, HALVES, FEATS], U32, align_bytes=64)
-            feat_planes = sample_pool.tile([P, HALVES, FEATS], U8, align_bytes=64)
-            feat_quantised[b] = (feat_codes, feat_planes)
+        def quantise_feat(b, halves):
+            if halves.start == 0:
+                feat_codes = sample_pool.tile([P, HALVES, FEATS], U32, align_bytes=64)
+                feat_planes = sample_pool.tile([P, HALVES, FEATS], U8, align_bytes=64)
+                feat_quantised[b] = (feat_codes, feat_planes)
+            codes, planes = feat_quantised[b]
             nc.vector.quantize_mx(
-                out=feat_codes[:].rearrange("p h c -> p (h c)").bitcast(FP8X4),
-                scales=feat_planes[:].rearrange("p h c -> p (h c)"),
-                in_=feat_grouped[b][:].rearrange("p h c t -> p (h c t)"),
+                out=codes[:, halves, :].rearrange("p h c -> p (h c)").bitcast(FP8X4),
+                scales=planes[:, halves, :].rearrange("p h c -> p (h c)"),
+                in_=feat_grouped[b][:, halves].rearrange("p h c t -> p (h c t)"),
             )
 
         def multiply_feat(b):
@@ -318,7 +322,7 @@ def tile_occurrencepool_pa_k_kernel(
             elif step == 3:
                 regroup_feat(b, 1)
             elif step == 4:
-                quantise_feat(b)
+                quantise_feat(b, slice(0, HALVES))
                 multiply_feat(b)
             elif step == 5:
                 take_mean(b)
@@ -357,7 +361,8 @@ def tile_occurrencepool_pa_k_kernel(
             transpose_feat(last, half)
         for half in range(HALVES):
             regroup_feat(last, half)
-        quantise_feat(last)
+        for half in range(HALVES):
+            quantise_feat(last, slice(half, half + 1))
         multiply_feat(last)
         take_mean(last)
         nc.sync.dma_start(out=out[SAMPLES - 1], in_=result[:, SAMPLES - 1, :])

@@ -23,12 +23,12 @@ VOXELS = 1024
 FEATS = 256
 MAPS = 128
 GROUPS = CHANNELS // K_PASS
+BOTH = (0, 1)
 HALVES = VOXELS // BANK
 FEAT_TILES = FEATS // P
 RUN = 4
 VECTOR_VOXELS = (464, 416)
-SCALAR_VOXELS = (432, 352)
-TENSOR_PIECE = 128
+SCALAR_VOXELS = (416, 368)
 WEIGHT_LOADS = 8
 OCC_LOAD_STEP = 4
 OCC_STEP = 8
@@ -125,9 +125,9 @@ def tile_occurrencepool_pa_k_kernel(
             for half in range(HALVES):
                 if step == first + half:
                     multiply_occ(b, half)
-                if step == first + half + 1:
+                if step == first + half + 1 and b < SAMPLES - 1:
                     take_abs(b, half)
-            if step == first + HALVES + 2:
+            if step == first + HALVES + 2 and b < SAMPLES - 1:
                 quantise_occ(b)
 
         occ_sums = {}
@@ -156,13 +156,7 @@ def tile_occurrencepool_pa_k_kernel(
         def load_chunk(b, g):
             raw = raw_pool.tile([P, PACK, VOXELS], BF16)
             rows = h_add[b, g * K_PASS : (g + 1) * K_PASS, :].rearrange("(p t) v -> p t v", t=PACK)
-            cuts = (
-                (slice(VECTOR_VOXELS[b], VOXELS), slice(0, VECTOR_VOXELS[b]))
-                if (b, g) == (0, 0)
-                else (slice(0, VOXELS),)
-            )
-            for voxels in cuts:
-                nc.sync.dma_start(out=raw[:, :, voxels], in_=rows[:, :, voxels])
+            nc.sync.dma_start(out=raw[:], in_=rows)
             raw_chunks[(b, g)] = raw
 
         inter_chunks = {}
@@ -171,18 +165,14 @@ def tile_occurrencepool_pa_k_kernel(
             raw = raw_chunks[(b, g)]
             first = VECTOR_VOXELS[b] + SCALAR_VOXELS[b]
             inter = inter_pool.tile([P, VOXELS - first, PACK], BF16, tag="inter", name="inter")
-            for start in range(0, VOXELS - first, TENSOR_PIECE):
-                voxels = slice(start, start + TENSOR_PIECE)
-                for t in range(0, PACK, 2):
-                    nc.tensor.matmul(
-                        out=inter[:, voxels, t : t + 2],
-                        lhsT=identity[:],
-                        rhs=raw[:, t : t + 2, first + voxels.start : first + voxels.stop].rearrange(
-                            "p t v -> p v t"
-                        ),
-                        start=True,
-                        stop=True,
-                    )
+            for t in range(0, PACK, 2):
+                nc.tensor.matmul(
+                    out=inter[:, :, t : t + 2],
+                    lhsT=identity[:],
+                    rhs=raw[:, t : t + 2, first:VOXELS].rearrange("p t v -> p v t"),
+                    start=True,
+                    stop=True,
+                )
             inter_chunks[(b, g)] = inter
 
         def regroup(b, g):
@@ -257,46 +247,46 @@ def tile_occurrencepool_pa_k_kernel(
                 bias=bias_cols[:, 1:2],
             )
 
-        def transpose_feat(b, half):
-            voxels = slice(half * BANK, (half + 1) * BANK)
+        def transpose_feat(b, halves, pool, tag):
             banks = []
             for j in range(FEAT_TILES):
-                if (b, half) == (SAMPLES - 1, HALVES - 1):
-                    turned = inter_pool.tile([P, 2, P], F32, tag="inter", name="turned")
-                else:
-                    turned = turn_pool.tile([P, 2, P], F32, tag="turn", name="turned")
-                words = feat_rounded[b][:, j, voxels].bitcast(F32)
-                for u in range(2):
-                    nc.tensor.transpose(turned[:, u, :], words[:, u::2], word_identity[:])
+                turned = pool.tile([P, len(halves), 2, P], F32, tag=tag, name="turned")
+                for i, half in enumerate(halves):
+                    voxels = slice(half * BANK, (half + 1) * BANK)
+                    words = feat_rounded[b][:, j, voxels].bitcast(F32)
+                    for u in range(2):
+                        nc.tensor.transpose(turned[:, i, u, :], words[:, u::2], word_identity[:])
                 banks.append(turned)
-            feat_turned[(b, half)] = banks
+            feat_turned[(b, halves)] = banks
 
-        def regroup_feat(b, half):
-            if half == 0:
+        def regroup_feat(b, halves):
+            if halves[0] == 0:
                 feat_grouped[b] = sample_pool.tile(
                     [P, HALVES, FEATS, PACK], BF16, name="feat_grouped", align_bytes=64
                 )
+            rows = slice(halves[0], halves[-1] + 1)
             for j, copy in enumerate((nc.vector.tensor_copy, nc.scalar.copy)):
                 copy(
-                    out=feat_grouped[b][:, half, P * j : P * (j + 1), :].bitcast(F32),
-                    in_=feat_turned[(b, half)][j][:].rearrange("p u c -> p c u"),
+                    out=feat_grouped[b][:, rows, P * j : P * (j + 1), :].bitcast(F32),
+                    in_=feat_turned[(b, halves)][j][:].rearrange("p h u c -> p h c u"),
                 )
 
         def quantise_feat(b, halves):
-            if halves.start == 0:
+            if halves[0] == 0:
                 feat_codes = sample_pool.tile([P, HALVES, FEATS], U32, align_bytes=64)
                 feat_planes = sample_pool.tile([P, HALVES, FEATS], U8, align_bytes=64)
                 feat_quantised[b] = (feat_codes, feat_planes)
+            rows = slice(halves[0], halves[-1] + 1)
             codes, planes = feat_quantised[b]
             nc.vector.quantize_mx(
-                out=codes[:, halves, :].rearrange("p h c -> p (h c)").bitcast(FP8X4),
-                scales=planes[:, halves, :].rearrange("p h c -> p (h c)"),
-                in_=feat_grouped[b][:, halves].rearrange("p h c t -> p (h c t)"),
+                out=codes[:, rows, :].rearrange("p h c -> p (h c)").bitcast(FP8X4),
+                scales=planes[:, rows, :].rearrange("p h c -> p (h c)"),
+                in_=feat_grouped[b][:, rows].rearrange("p h c t -> p (h c t)"),
             )
 
         def multiply_feat(b):
             codes, planes = feat_quantised[b]
-            pooled[b] = turn_pool.tile([P, FEATS], F32, tag="turn", name="pooled")
+            pooled[b] = sum_pool.tile([P, FEATS], F32, name="sum%d0" % b)
             for half in range(HALVES):
                 nc.tensor.matmul_mx(
                     out=pooled[b][:],
@@ -315,17 +305,9 @@ def tile_occurrencepool_pa_k_kernel(
             if step == 1:
                 add_bias(b, 0)
                 add_bias(b, 1)
-                transpose_feat(b, 0)
+                transpose_feat(b, BOTH, turn_pool, "turn")
             elif step == 2:
-                regroup_feat(b, 0)
-                transpose_feat(b, 1)
-            elif step == 3:
-                regroup_feat(b, 1)
-            elif step == 4:
-                quantise_feat(b, slice(0, HALVES))
-                multiply_feat(b)
-            elif step == 5:
-                take_mean(b)
+                regroup_feat(b, BOTH)
 
         chunks = [(b, g) for b in range(SAMPLES) for g in range(GROUPS)]
         waiting = None
@@ -353,16 +335,20 @@ def tile_occurrencepool_pa_k_kernel(
                 quantise_and_multiply(*waiting)
             waiting = (b, g, grouped)
         quantise_and_multiply(*waiting)
-        for b in range(SAMPLES - 1):
-            nc.sync.dma_start(out=out[b], in_=result[:, b, :])
         last = SAMPLES - 1
         for half in range(HALVES):
-            add_bias(last, half)
-            transpose_feat(last, half)
+            take_abs(last, half)
+        add_bias(last, 0)
+        transpose_feat(last, (0,), turn_pool, "turn")
+        add_bias(last, 1)
+        transpose_feat(last, (1,), inter_pool, "inter")
+        quantise_occ(last)
+        regroup_feat(last, (0,))
+        quantise_feat(0, BOTH)
+        regroup_feat(last, (1,))
         for half in range(HALVES):
-            regroup_feat(last, half)
-        for half in range(HALVES):
-            quantise_feat(last, slice(half, half + 1))
-        multiply_feat(last)
-        take_mean(last)
-        nc.sync.dma_start(out=out[SAMPLES - 1], in_=result[:, SAMPLES - 1, :])
+            quantise_feat(last, (half,))
+        for b in range(SAMPLES):
+            multiply_feat(b)
+            take_mean(b)
+            nc.sync.dma_start(out=out[b], in_=result[:, b, :])

@@ -233,16 +233,17 @@ def tile_occurrencepool_pa_k_kernel(
 
         def add_bias(b, half):
             if half == 0:
-                feat_rounded[b] = sample_pool.tile([P, FEAT_TILES, VOXELS], BF16, name="feat_rounded")
-            voxels = slice(half * BANK, (half + 1) * BANK)
+                feat_rounded[b] = sample_pool.tile(
+                    [P, FEAT_TILES, HALVES, 2, P, 2], BF16, name="feat_rounded"
+                )
             nc.vector.tensor_scalar_add(
-                out=feat_rounded[b][:, 0, voxels],
-                in0=feat_sums[b][0][half][:],
+                out=feat_rounded[b][:, 0, half],
+                in0=feat_sums[b][0][half][:].rearrange("c (p u e) -> c u p e", u=2, e=2),
                 scalar1=bias_cols[:, 0:1],
             )
             nc.scalar.activation(
-                out=feat_rounded[b][:, 1, voxels],
-                in_=feat_sums[b][1][half][:],
+                out=feat_rounded[b][:, 1, half],
+                in_=feat_sums[b][1][half][:].rearrange("c (p u e) -> c u p e", u=2, e=2),
                 func=ACT.Identity,
                 bias=bias_cols[:, 1:2],
             )
@@ -252,10 +253,9 @@ def tile_occurrencepool_pa_k_kernel(
             for j in range(FEAT_TILES):
                 turned = pool.tile([P, len(halves), 2, P], F32, tag=tag, name="turned")
                 for i, half in enumerate(halves):
-                    voxels = slice(half * BANK, (half + 1) * BANK)
-                    words = feat_rounded[b][:, j, voxels].bitcast(F32)
                     for u in range(2):
-                        nc.tensor.transpose(turned[:, i, u, :], words[:, u::2], word_identity[:])
+                        words = feat_rounded[b][:, j, half, u].rearrange("c p e -> c (p e)")
+                        nc.tensor.transpose(turned[:, i, u, :], words.bitcast(F32), word_identity[:])
                 banks.append(turned)
             feat_turned[(b, halves)] = banks
 
@@ -286,20 +286,27 @@ def tile_occurrencepool_pa_k_kernel(
 
         def multiply_feat(b):
             codes, planes = feat_quantised[b]
-            pooled[b] = sum_pool.tile([P, FEATS], F32, name="sum%d0" % b)
-            for half in range(HALVES):
-                nc.tensor.matmul_mx(
-                    out=pooled[b][:],
-                    lhsT=occ_codes[:, b, half, :].bitcast(FP8X4),
-                    lhsT_scale=occ_planes[:, b, half, :],
-                    rhs=codes[:, half, :].bitcast(FP8X4),
-                    rhs_scale=planes[:, half, :],
-                    start=(half == 0),
-                    stop=(half == HALVES - 1),
-                )
+            pooled[b] = [
+                sum_pool.tile([P, P], F32, name="sum%d%d" % (j, b)) for j in range(FEAT_TILES)
+            ]
+            for j in range(FEAT_TILES):
+                channels = slice(P * j, P * (j + 1))
+                for half in range(HALVES):
+                    nc.tensor.matmul_mx(
+                        out=pooled[b][j][:],
+                        lhsT=occ_codes[:, b, half, :].bitcast(FP8X4),
+                        lhsT_scale=occ_planes[:, b, half, :],
+                        rhs=codes[:, half, channels].bitcast(FP8X4),
+                        rhs_scale=planes[:, half, channels],
+                        start=(half == 0),
+                        stop=(half == HALVES - 1),
+                    )
 
         def take_mean(b):
-            nc.scalar.mul(out=result[:, b, :], in_=pooled[b][:], mul=1.0 / VOXELS)
+            nc.vector.tensor_scalar_mul(
+                out=result[:, b, 0:P], in0=pooled[b][0][:], scalar1=1.0 / VOXELS
+            )
+            nc.scalar.mul(out=result[:, b, P:FEATS], in_=pooled[b][1][:], mul=1.0 / VOXELS)
 
         def pool_step(b, step):
             if step == 1:
@@ -325,7 +332,8 @@ def tile_occurrencepool_pa_k_kernel(
                 nc.sync.dma_start(out=h_occ_sb[:, b, :], in_=h_occ[b])
             if step + 2 < len(chunks):
                 load_chunk(*chunks[step + 2])
-            if step + 1 < len(chunks):
+            ahead = step > GROUPS
+            if ahead and step + 1 < len(chunks):
                 regroup_on_tensor(*chunks[step + 1])
             grouped = regroup(b, g)
             occ_step(b, g)
@@ -333,6 +341,8 @@ def tile_occurrencepool_pa_k_kernel(
                 pool_step(b - 1, g)
             if waiting is not None:
                 quantise_and_multiply(*waiting)
+            if not ahead:
+                regroup_on_tensor(*chunks[step + 1])
             waiting = (b, g, grouped)
         quantise_and_multiply(*waiting)
         last = SAMPLES - 1

@@ -27,8 +27,8 @@ BOTH = (0, 1)
 HALVES = VOXELS // BANK
 FEAT_TILES = FEATS // P
 RUN = 4
-VECTOR_VOXELS = (464, 416)
-SCALAR_VOXELS = (416, 368)
+VECTOR_VOXELS = (456, 424)
+SCALAR_VOXELS = (408, 376)
 WEIGHT_LOADS = 8
 OCC_LOAD_STEP = 4
 OCC_STEP = 8
@@ -318,8 +318,8 @@ def tile_occurrencepool_pa_k_kernel(
 
         chunks = [(b, g) for b in range(SAMPLES) for g in range(GROUPS)]
         waiting = None
-        load_chunk(*chunks[0])
-        load_chunk(*chunks[1])
+        for chunk in chunks[:3]:
+            load_chunk(*chunk)
         regroup_on_tensor(*chunks[0])
         for step, (b, g) in enumerate(chunks):
             if step == 0:
@@ -330,10 +330,9 @@ def tile_occurrencepool_pa_k_kernel(
                 if b == 0:
                     load_small_weights()
                 nc.sync.dma_start(out=h_occ_sb[:, b, :], in_=h_occ[b])
-            if step + 2 < len(chunks):
-                load_chunk(*chunks[step + 2])
-            ahead = step > GROUPS
-            if ahead and step + 1 < len(chunks):
+            if step + 3 < len(chunks):
+                load_chunk(*chunks[step + 3])
+            if step + 1 < len(chunks):
                 regroup_on_tensor(*chunks[step + 1])
             grouped = regroup(b, g)
             occ_step(b, g)
@@ -341,8 +340,6 @@ def tile_occurrencepool_pa_k_kernel(
                 pool_step(b - 1, g)
             if waiting is not None:
                 quantise_and_multiply(*waiting)
-            if not ahead:
-                regroup_on_tensor(*chunks[step + 1])
             waiting = (b, g, grouped)
         quantise_and_multiply(*waiting)
         last = SAMPLES - 1

from contextlib import ExitStack

import concourse.mybir as mybir
from concourse.masks import make_identity

BF16 = mybir.dt.bfloat16
F32 = mybir.dt.float32
I32 = mybir.dt.int32
U32 = mybir.dt.uint32
U8 = mybir.dt.uint8
FP8X4 = mybir.dt.float8_e4m3fn_x4
FP4X4 = mybir.dt.float4_e2m1fn_x4
ACT = mybir.ActivationFunctionType

P = 128
PACK = 4
K_PASS = P * PACK
BANK = 512

SAMPLES = 2
CHANNELS = 8192
VOXELS = 1024
FEATS = 256
MAPS = 128
GROUPS = CHANNELS // K_PASS
BOTH = (0, 1)
HALVES = VOXELS // BANK
FEAT_TILES = FEATS // P
RUN = 4
VECTOR_VOXELS = (456, 424)
SCALAR_VOXELS = (408, 376)
WEIGHT_LOADS = 8
OCC_LOAD_STEP = 4
OCC_STEP = 8
RAW_BUFS = 8
CODE_BUFS = 6

FLOPS = 2 * SAMPLES * VOXELS * (FEATS * CHANNELS + MAPS * P + MAPS * FEATS)


def tile_occurrencepool_pa_k_kernel(
    tc, h_add, w_add2_words, w_add2_scales, b_add2, h_occ, w_occ3, out
):
    nc = tc.nc
    with ExitStack() as stack:
        stack.enter_context(tc.manual_schedule())
        keep = stack.enter_context(tc.tile_pool(name="keep", bufs=1))
        raw_pool = stack.enter_context(tc.tile_pool(name="raw", bufs=RAW_BUFS))
        chunk_pool = stack.enter_context(tc.tile_pool(name="chunk", bufs=3))
        codes_pool = stack.enter_context(tc.tile_pool(name="codes", bufs=CODE_BUFS))
        sample_pool = stack.enter_context(tc.tile_pool(name="sample", bufs=2))
        sum_pool = stack.enter_context(tc.psum_pool(name="sums", bufs=1))
        turn_pool = stack.enter_context(tc.psum_pool(name="turn", bufs=2))
        inter_pool = stack.enter_context(tc.psum_pool(name="inter", bufs=2))

        w_words = keep.tile([P, GROUPS, 2 * FEATS], U8, align_bytes=64)
        w_planes = keep.tile([P, GROUPS, FEATS], U8, align_bytes=64)
        identity = keep.tile([P, P], BF16)
        word_identity = keep.tile([P, P], F32)
        w_occ_sb = keep.tile([P, P], BF16)
        w_occ_t = keep.tile([P, P], BF16)
        h_occ_sb = keep.tile([P, SAMPLES, VOXELS], BF16)
        bias_rows = keep.tile([P, P], BF16)
        bias_cols = keep.tile([P, FEAT_TILES], F32)
        occ_grouped = keep.tile([P, SAMPLES, HALVES, MAPS, PACK], BF16, align_bytes=64)
        occ_codes = keep.tile([P, SAMPLES, HALVES, MAPS], U32, align_bytes=64)
        occ_planes = keep.tile([P, SAMPLES, HALVES, MAPS], U8, align_bytes=64)
        result = keep.tile([P, SAMPLES, FEATS], F32)
        warm = keep.tile([P, 1], F32)
        warm_out = keep.tile([P, 1], F32)

        nc.gpsimd.memset(warm[:], 0.0)
        nc.scalar.activation(out=warm_out[:], in_=warm[:], func=ACT.Abs)
        nc.vector.memset(w_planes[:].rearrange("p g n -> p (g n)").bitcast(I32), 0)
        nc.vector.memset(bias_rows[:], 0.0)
        make_identity(nc, identity[:])
        make_identity(nc, word_identity[:])

        def load_weight_scales():
            scale_rows = w_add2_scales.rearrange("g (q r) n -> r q g n", r=PACK)
            for r in range(PACK):
                nc.sync.dma_start(
                    out=w_planes[r:P:32, :, :].bitcast(I32), in_=scale_rows[r].bitcast(I32)
                )

        def load_weight_words(first_group):
            groups = slice(first_group, first_group + GROUPS // WEIGHT_LOADS)
            nc.sync.dma_start(
                out=w_words[:, groups, :].bitcast(I32),
                in_=w_add2_words[groups].rearrange("g p w -> p g w").bitcast(I32),
            )

        def load_small_weights():
            nc.sync.dma_start(out=w_occ_sb[:], in_=w_occ3)
            nc.sync.dma_start(
                out=bias_rows[0:FEAT_TILES, :], in_=b_add2.rearrange("(j c) -> j c", j=FEAT_TILES)
            )

        turned_weights = []

        def turn_small_weights():
            for rows in (bias_rows, w_occ_sb):
                turned = turn_pool.tile([P, P], BF16, tag="turn", name="turned_weight")
                nc.tensor.transpose(turned[:], rows[:], identity[:])
                turned_weights.append(turned)

        def copy_small_weights():
            bias_ps, w_occ_ps = turned_weights
            nc.vector.tensor_copy(out=bias_cols[:], in_=bias_ps[:, 0:FEAT_TILES])
            nc.vector.tensor_copy(out=w_occ_t[:], in_=w_occ_ps[:])

        def quantise_occ(b):
            nc.vector.quantize_mx(
                out=occ_codes[:, b].rearrange("p h o -> p (h o)").bitcast(FP8X4),
                scales=occ_planes[:, b].rearrange("p h o -> p (h o)"),
                in_=occ_grouped[:, b].rearrange("p h o t -> p (h o t)"),
            )

        def occ_step(b, step):
            first = OCC_STEP if b > 0 else OCC_STEP + 2
            if step == OCC_STEP and b == 0:
                turn_small_weights()
            if step == OCC_STEP + 1 and b == 0:
                copy_small_weights()
            for half in range(HALVES):
                if step == first + half:
                    multiply_occ(b, half)
                if step == first + half + 1 and b < SAMPLES - 1:
                    take_abs(b, half)
            if step == first + HALVES + 2 and b < SAMPLES - 1:
                quantise_occ(b)

        occ_sums = {}

        def multiply_occ(b, half):
            occ_ps = turn_pool.tile([P, PACK, MAPS], F32, tag="turn", name="occ_ps")
            for t in range(PACK):
                nc.tensor.matmul(
                    out=occ_ps[:, t, :],
                    lhsT=h_occ_sb[:, b, half * K_PASS + t : (half + 1) * K_PASS : PACK],
                    rhs=w_occ_t[:],
                    start=True,
                    stop=True,
                )
            occ_sums[(b, half)] = occ_ps

        def take_abs(b, half):
            nc.scalar.activation(
                out=occ_grouped[:, b, half],
                in_=occ_sums[(b, half)][:].rearrange("p t o -> p o t"),
                func=ACT.Abs,
            )

        raw_chunks = {}

        def load_chunk(b, g):
            raw = raw_pool.tile([P, PACK, VOXELS], BF16)
            rows = h_add[b, g * K_PASS : (g + 1) * K_PASS, :].rearrange("(p t) v -> p t v", t=PACK)
            nc.sync.dma_start(out=raw[:], in_=rows)
            raw_chunks[(b, g)] = raw

        inter_chunks = {}

        def regroup_on_tensor(b, g):
            raw = raw_chunks[(b, g)]
            first = VECTOR_VOXELS[b] + SCALAR_VOXELS[b]
            inter = inter_pool.tile([P, VOXELS - first, PACK], BF16, tag="inter", name="inter")
            for t in range(0, PACK, 2):
                nc.tensor.matmul(
                    out=inter[:, :, t : t + 2],
                    lhsT=identity[:],
                    rhs=raw[:, t : t + 2, first:VOXELS].rearrange("p t v -> p v t"),
                    start=True,
                    stop=True,
                )
            inter_chunks[(b, g)] = inter

        def regroup(b, g):
            raw = raw_chunks[(b, g)]
            grouped = chunk_pool.tile([P, VOXELS, PACK], BF16, align_bytes=64)
            scalar_end = VECTOR_VOXELS[b] + SCALAR_VOXELS[b]
            shares = (
                (nc.vector.tensor_copy, slice(0, VECTOR_VOXELS[b])),
                (nc.scalar.copy, slice(VECTOR_VOXELS[b], scalar_end)),
            )
            for copy, voxels in shares:
                copy(
                    out=grouped[:, voxels, :].rearrange("p (c i) t -> p c t i", i=RUN),
                    in_=raw[:, :, voxels].rearrange("p t (c i) -> p c t i", i=RUN),
                )
            nc.scalar.copy(out=grouped[:, scalar_end:VOXELS, :], in_=inter_chunks[(b, g)][:])
            return grouped

        feat_sums = {}

        def quantise_and_multiply(b, g, grouped):
            if g == 0:
                feat_sums[b] = [
                    [
                        sum_pool.tile([P, BANK], F32, name="sum%d%d" % (j, half))
                        for half in range(HALVES)
                    ]
                    for j in range(FEAT_TILES)
                ]
            codes = codes_pool.tile([P, VOXELS], U32, align_bytes=64)
            plane = codes_pool.tile([P, VOXELS], U8, align_bytes=64)
            pieces = HALVES if g == GROUPS - 1 or (b, g) == (SAMPLES - 1, GROUPS - 2) else 1
            for piece in range(pieces):
                voxels = slice(piece * VOXELS // pieces, (piece + 1) * VOXELS // pieces)
                nc.vector.quantize_mx(
                    out=codes[:, voxels].bitcast(FP8X4),
                    scales=plane[:, voxels],
                    in_=grouped[:, voxels, :].rearrange("p v t -> p (v t)"),
                )
            for half in range(HALVES):
                voxels = slice(half * BANK, (half + 1) * BANK)
                for j in range(FEAT_TILES):
                    nc.tensor.matmul_mx(
                        out=feat_sums[b][j][half][:],
                        lhsT=w_words[:, g, 2 * P * j : 2 * P * (j + 1)].bitcast(FP4X4),
                        lhsT_scale=w_planes[:, g, P * j : P * (j + 1)],
                        rhs=codes[:, voxels].bitcast(FP8X4),
                        rhs_scale=plane[:, voxels],
                        start=(g == 0),
                        stop=(g == GROUPS - 1),
                    )

        feat_rounded = {}
        feat_turned = {}
        feat_grouped = {}
        feat_quantised = {}
        pooled = {}

        def add_bias(b, half):
            if half == 0:
                feat_rounded[b] = sample_pool.tile(
                    [P, FEAT_TILES, HALVES, 2, P, 2], BF16, name="feat_rounded"
                )
            nc.vector.tensor_scalar_add(
                out=feat_rounded[b][:, 0, half],
                in0=feat_sums[b][0][half][:].rearrange("c (p u e) -> c u p e", u=2, e=2),
                scalar1=bias_cols[:, 0:1],
            )
            nc.scalar.activation(
                out=feat_rounded[b][:, 1, half],
                in_=feat_sums[b][1][half][:].rearrange("c (p u e) -> c u p e", u=2, e=2),
                func=ACT.Identity,
                bias=bias_cols[:, 1:2],
            )

        def transpose_feat(b, halves, pool, tag):
            banks = []
            for j in range(FEAT_TILES):
                turned = pool.tile([P, len(halves), 2, P], F32, tag=tag, name="turned")
                for i, half in enumerate(halves):
                    for u in range(2):
                        words = feat_rounded[b][:, j, half, u].rearrange("c p e -> c (p e)")
                        nc.tensor.transpose(turned[:, i, u, :], words.bitcast(F32), word_identity[:])
                banks.append(turned)
            feat_turned[(b, halves)] = banks

        def regroup_feat(b, halves):
            if halves[0] == 0:
                feat_grouped[b] = sample_pool.tile(
                    [P, HALVES, FEATS, PACK], BF16, name="feat_grouped", align_bytes=64
                )
            rows = slice(halves[0], halves[-1] + 1)
            for j, copy in enumerate((nc.vector.tensor_copy, nc.scalar.copy)):
                copy(
                    out=feat_grouped[b][:, rows, P * j : P * (j + 1), :].bitcast(F32),
                    in_=feat_turned[(b, halves)][j][:].rearrange("p h u c -> p h c u"),
                )

        def quantise_feat(b, halves):
            if halves[0] == 0:
                feat_codes = sample_pool.tile([P, HALVES, FEATS], U32, align_bytes=64)
                feat_planes = sample_pool.tile([P, HALVES, FEATS], U8, align_bytes=64)
                feat_quantised[b] = (feat_codes, feat_planes)
            rows = slice(halves[0], halves[-1] + 1)
            codes, planes = feat_quantised[b]
            nc.vector.quantize_mx(
                out=codes[:, rows, :].rearrange("p h c -> p (h c)").bitcast(FP8X4),
                scales=planes[:, rows, :].rearrange("p h c -> p (h c)"),
                in_=feat_grouped[b][:, rows].rearrange("p h c t -> p (h c t)"),
            )

        def multiply_feat(b):
            codes, planes = feat_quantised[b]
            pooled[b] = [
                sum_pool.tile([P, P], F32, name="sum%d%d" % (j, b)) for j in range(FEAT_TILES)
            ]
            for j in range(FEAT_TILES):
                channels = slice(P * j, P * (j + 1))
                for half in range(HALVES):
                    nc.tensor.matmul_mx(
                        out=pooled[b][j][:],
                        lhsT=occ_codes[:, b, half, :].bitcast(FP8X4),
                        lhsT_scale=occ_planes[:, b, half, :],
                        rhs=codes[:, half, channels].bitcast(FP8X4),
                        rhs_scale=planes[:, half, channels],
                        start=(half == 0),
                        stop=(half == HALVES - 1),
                    )

        def take_mean(b):
            nc.vector.tensor_scalar_mul(
                out=result[:, b, 0:P], in0=pooled[b][0][:], scalar1=1.0 / VOXELS
            )
            nc.scalar.mul(out=result[:, b, P:FEATS], in_=pooled[b][1][:], mul=1.0 / VOXELS)

        def pool_step(b, step):
            if step == 1:
                add_bias(b, 0)
                add_bias(b, 1)
                transpose_feat(b, BOTH, turn_pool, "turn")
            elif step == 2:
                regroup_feat(b, BOTH)

        chunks = [(b, g) for b in range(SAMPLES) for g in range(GROUPS)]
        waiting = None
        for chunk in chunks[:3]:
            load_chunk(*chunk)
        regroup_on_tensor(*chunks[0])
        for step, (b, g) in enumerate(chunks):
            if step == 0:
                load_weight_scales()
            if b == 0 and g % (GROUPS // WEIGHT_LOADS) == 0:
                load_weight_words(g)
            if g == OCC_LOAD_STEP:
                if b == 0:
                    load_small_weights()
                nc.sync.dma_start(out=h_occ_sb[:, b, :], in_=h_occ[b])
            if step + 3 < len(chunks):
                load_chunk(*chunks[step + 3])
            if step + 1 < len(chunks):
                regroup_on_tensor(*chunks[step + 1])
            grouped = regroup(b, g)
            occ_step(b, g)
            if b > 0:
                pool_step(b - 1, g)
            if waiting is not None:
                quantise_and_multiply(*waiting)
            waiting = (b, g, grouped)
        quantise_and_multiply(*waiting)
        last = SAMPLES - 1
        for half in range(HALVES):
            take_abs(last, half)
        add_bias(last, 0)
        transpose_feat(last, (0,), turn_pool, "turn")
        add_bias(last, 1)
        transpose_feat(last, (1,), inter_pool, "inter")
        quantise_occ(last)
        regroup_feat(last, (0,))
        quantise_feat(0, BOTH)
        regroup_feat(last, (1,))
        for half in range(HALVES):
            quantise_feat(last, (half,))
        for b in range(SAMPLES):
            multiply_feat(b)
            take_mean(b)
            nc.sync.dma_start(out=out[b], in_=result[:, b, :])
